import numpy as np
import ml_dtypes


def mxq(x, axis, fmt="e4m3"):
    dtype, down = {"e4m3": (ml_dtypes.float8_e4m3fn, 7), "e5m2": (ml_dtypes.float8_e5m2, 14)}[fmt]
    v = np.moveaxis(np.asarray(x, np.float32).astype(ml_dtypes.bfloat16).astype(np.float64), axis, -1)
    blocks = v.reshape(v.shape[:-1] + (-1, 32))
    amax = np.abs(blocks).max(-1, keepdims=True)
    byte = np.maximum(np.where(amax > 0, np.frexp(amax)[1] - 1 + 127, 0) - down, 1)
    scale = np.exp2(byte - 127.0)
    codes = (blocks / scale).astype(np.float32).astype(dtype).astype(np.float64)
    return np.moveaxis((codes * scale).reshape(v.shape), -1, axis)


WIDE = False


def mx_kscale(k):
    if not WIDE:
        return np.ones(k)
    levels = np.array([10, -10, 5, -5, 0])
    a = np.random.permutation(np.resize(levels, k // 512 * 4)).reshape(k // 512, 4)
    idx = np.arange(k)
    return np.exp2(a[idx // 512, idx % 128 // 32])


BF16 = ml_dtypes.bfloat16


def bf(x):
    return np.asarray(x, np.float32).astype(BF16)


def f64(x):
    return np.asarray(x).astype(np.float64)


B, S, D, H, DH = 1, 1024, 1024, 8, 128
E = H * DH
EPS = 1e-12


def rotate_half(t):
    t1, t2 = np.split(t, 2, axis=-1)
    return np.concatenate((-t2, t1), axis=-1)


def apply_rotary(pos, t):
    return t * np.cos(pos) + rotate_half(t) * np.sin(pos)


def setup_inputs():
    s = mx_kscale(D)
    ang = np.random.uniform(-np.pi, np.pi, (S, DH // 2))
    col = np.concatenate((np.full(E, np.sqrt(3.0 / DH)), np.full(E, np.sqrt(3.0 / DH)), np.ones(E)))
    return {"x": bf(np.random.standard_normal((B, S, D))),
            "rotary_emb": bf(np.concatenate((ang, ang), axis=-1)),
            "gamma": bf((1.0 + 0.1 * np.random.standard_normal(D)) * s),
            "w_qkv": bf(np.random.standard_normal((D, 3 * E)) * col / np.sqrt(D) / s[:, None])}


def reference(x, rotary_emb, gamma, w_qkv):
    x, pos = f64(x), f64(rotary_emb)
    l2 = np.sqrt((x * x).sum(-1, keepdims=True))
    xn = x / np.maximum(l2, EPS) * np.sqrt(D) * f64(gamma)
    qkv = mxq(xn, 2, "e4m3") @ mxq(f64(w_qkv), 0, "e4m3")
    qkv = qkv.reshape(B, S, 3, H, DH).transpose(2, 0, 3, 1, 4)
    q, k, v = qkv[0], qkv[1], qkv[2]
    q = apply_rotary(pos, q)
    k = apply_rotary(pos, k)
    q = q * np.sqrt(DH)
    return q, k, v

@@ -1,0 +1,193 @@
+import math
+from contextlib import ExitStack
+
+import concourse.mybir as mybir
+from concourse.masks import make_identity
+
+FP8X4 = mybir.dt.float8_e4m3fn_x4
+BF16 = mybir.dt.bfloat16
+F32 = mybir.dt.float32
+U32 = mybir.dt.uint32
+U8 = mybir.dt.uint8
+ACT = mybir.ActivationFunctionType
+ALU = mybir.AluOpType
+
+P = 128
+SEQ = 1024
+DIM = 1024
+HEADS = 8
+DH = 128
+HALF = DH // 2
+EPS = 1e-12
+
+PACK = 4
+K_PASS = P * PACK
+PASSES = DIM // K_PASS
+K_CHUNKS = DIM // P
+ROW_TILES = SEQ // P
+N_COLS = 512
+GROUP_HEADS = N_COLS // DH
+T_RUN = 4
+
+GROUPS = ((0, 0), (0, 1), (2, 0), (1, 0), (2, 1), (1, 1))
+
+FLOPS = 2 * SEQ * DIM * 3 * HEADS * DH
+
+
+def tile_ringattention_pa_kernel(tc, x, rotary_emb, gamma, w_qkv, out_q, out_k, out_v):
+    nc = tc.nc
+    outs = (out_q, out_k, out_v)
+    with ExitStack() as ctx:
+        keep = ctx.enter_context(tc.tile_pool(name="keep", bufs=1))
+        squares = ctx.enter_context(tc.tile_pool(name="squares", bufs=2))
+        normed = ctx.enter_context(tc.tile_pool(name="normed", bufs=3))
+        w_in = ctx.enter_context(tc.tile_pool(name="w_in", bufs=len(GROUPS)))
+        w_words = ctx.enter_context(tc.tile_pool(name="w_words", bufs=3))
+        w_mx = ctx.enter_context(tc.tile_pool(name="w_mx", bufs=3))
+        products = ctx.enter_context(tc.tile_pool(name="products", bufs=3))
+        results = ctx.enter_context(tc.tile_pool(name="results", bufs=4))
+        psum = ctx.enter_context(tc.psum_pool(name="psum", bufs=8))
+
+        angles = keep.tile([P, ROW_TILES, DH], BF16)
+        nc.sync.dma_start(out=angles[:], in_=rotary_emb.rearrange("(p t) d -> p t d", t=ROW_TILES))
+        gamma_row = keep.tile([P, DIM], BF16)
+        nc.vector.memset(gamma_row[:], 0.0)
+        nc.sync.dma_start(out=gamma_row[0:1, :], in_=gamma.rearrange("(o k) -> o k", o=1))
+        x_rows = keep.tile([P, ROW_TILES, DIM], BF16)
+        x_view = x[0].rearrange("(p t) k -> p t k", t=ROW_TILES)
+        w_view = w_qkv.rearrange("(c p) n -> p c n", p=P)
+        w_raw = {}
+
+        def load_x(t):
+            nc.sync.dma_start(out=x_rows[:, t : t + 2, :], in_=x_view[:, t : t + 2, :])
+
+        def load_w(section, half):
+            first = (section * 2 + half) * N_COLS
+            w_raw[(section, half)] = w_in.tile([P, K_CHUNKS, N_COLS], BF16, name="w_raw")
+            nc.sync.dma_start(out=w_raw[(section, half)][:], in_=w_view[:, :, first : first + N_COLS])
+
+        load_x(0)
+        load_w(*GROUPS[0])
+        for t in range(2, ROW_TILES, 2):
+            load_x(t)
+        for section, half in GROUPS[1:]:
+            load_w(section, half)
+
+        ident = keep.tile([P, P], BF16)
+        make_identity(nc, ident[:])
+        ones = keep.tile([P, P], BF16)
+        nc.vector.memset(ones[:], 1.0)
+        minus_half = keep.tile([P, ROW_TILES], F32)
+        nc.gpsimd.memset(minus_half[:], -0.5)
+
+        table_k = keep.tile([P, ROW_TILES, 2, DH], F32)
+        table_q = keep.tile([P, ROW_TILES, 2, DH], F32)
+        sin_half = keep.tile([P, ROW_TILES, DH], F32)
+        nc.scalar.activation(out=sin_half[:], in_=angles[:], func=ACT.Sin, scale=0.5)
+        nc.scalar.activation(out=table_k[:, :, 1, 0:HALF], in_=angles[:, :, HALF:DH], func=ACT.Sin)
+        nc.scalar.activation(out=table_k[:, :, 1, HALF:DH], in_=angles[:, :, 0:HALF], func=ACT.Sin, scale=-1.0)
+        tables = (table_q, table_k)
+
+        gamma_all = keep.tile([P, DIM], BF16)
+        for n in range(0, DIM, N_COLS):
+            spread = psum.tile([P, N_COLS], F32, tag="bank")
+            nc.tensor.matmul(out=spread[:], lhsT=ones[:], rhs=gamma_row[:, n : n + N_COLS], start=True, stop=True)
+            nc.vector.tensor_copy(out=gamma_all[:, n : n + N_COLS], in_=spread[:])
+
+        x_codes = keep.tile([P, ROW_TILES, PASSES, P], U32, align_bytes=64)
+        x_scales = keep.tile([P, ROW_TILES, PASSES, P], U8, align_bytes=64)
+        mean_sq = keep.tile([P, ROW_TILES], F32)
+        floored = keep.tile([P, ROW_TILES], F32)
+        inv_rms = keep.tile([P, ROW_TILES], F32)
+        for t in range(ROW_TILES):
+            sq = squares.tile([P, DIM], BF16)
+            nc.scalar.activation(
+                out=sq[:], in_=x_rows[:, t, :], func=ACT.Square, scale=1.0 / math.sqrt(DIM),
+                accum_out=mean_sq[:, t : t + 1],
+            )
+            nc.gpsimd.tensor_scalar(
+                out=floored[:, t : t + 1], in0=mean_sq[:, t : t + 1], scalar1=EPS * EPS / DIM, scalar2=None,
+                op0=ALU.max,
+            )
+            nc.gpsimd.tensor_tensor(
+                out=inv_rms[:, t : t + 1], in0=floored[:, t : t + 1], in1=minus_half[:, t : t + 1], op=ALU.pow
+            )
+            xn = normed.tile([P, DIM], BF16)
+            nc.vector.scalar_tensor_tensor(
+                out=xn[:], in0=x_rows[:, t, :], scalar=inv_rms[:, t : t + 1], in1=gamma_all[:],
+                op0=ALU.mult, op1=ALU.mult,
+            )
+            xn_t = psum.tile([P, K_CHUNKS, P], BF16, tag="bank")
+            for c in range(K_CHUNKS):
+                nc.tensor.transpose(xn_t[:, c, :], xn[:, c * P : (c + 1) * P], ident[:])
+            xn_words = normed.tile([P, PASSES, P, PACK], BF16, align_bytes=64)
+            nc.scalar.copy(out=xn_words[:], in_=xn_t[:].rearrange("p (g u) r -> p g r u", u=PACK))
+            nc.vector.quantize_mx(
+                out=x_codes[:, t].rearrange("p g r -> p (g r)").bitcast(FP8X4),
+                scales=x_scales[:, t].rearrange("p g r -> p (g r)"),
+                in_=xn_words[:].rearrange("p g r u -> p (g r u)"),
+            )
+
+        nc.vector.tensor_tensor(out=sin_half[:], in0=sin_half[:], in1=sin_half[:], op=ALU.mult)
+        nc.vector.tensor_scalar(
+            out=table_k[:, :, 0, :], in0=sin_half[:], scalar1=-2.0, scalar2=1.0, op0=ALU.mult, op1=ALU.add
+        )
+        nc.vector.tensor_scalar_mul(out=table_q[:], in0=table_k[:], scalar1=math.sqrt(DH))
+
+        for index, (section, half) in enumerate(GROUPS):
+            w_codes = w_mx.tile([P, PASSES, N_COLS], U32, align_bytes=64)
+            w_scales = w_mx.tile([P, PASSES, N_COLS], U8, align_bytes=64)
+            for g in range(PASSES):
+                grouped = w_words.tile([P, N_COLS, PACK], BF16, align_bytes=64)
+                regroup = nc.vector.tensor_copy if index == 0 else nc.scalar.copy
+                regroup(
+                    out=grouped[:].rearrange("p (c i) u -> p c u i", i=4),
+                    in_=w_raw[(section, half)][:, g * PACK : (g + 1) * PACK, :].rearrange("p u (c i) -> p c u i", i=4),
+                )
+                nc.vector.quantize_mx(
+                    out=w_codes[:, g, :].bitcast(FP8X4),
+                    scales=w_scales[:, g, :],
+                    in_=grouped[:].rearrange("p n u -> p (n u)"),
+                )
+            out_view = outs[section][0].rearrange("h (p t) d -> p h t d", t=ROW_TILES)
+            first_head = half * GROUP_HEADS
+            for t0 in range(0, ROW_TILES, T_RUN):
+                result = results.tile([P, GROUP_HEADS, T_RUN, DH], F32)
+                if section < 2:
+                    product = products.tile([P, T_RUN, 2, GROUP_HEADS, DH], F32)
+                for j in range(T_RUN):
+                    t = t0 + j
+                    acc = psum.tile([P, N_COLS], F32, tag="bank")
+                    for g in range(PASSES):
+                        nc.tensor.matmul_mx(
+                            out=acc[:],
+                            lhsT=x_codes[:, t, g, :].bitcast(FP8X4),
+                            lhsT_scale=x_scales[:, t, g, :],
+                            rhs=w_codes[:, g, :].bitcast(FP8X4),
+                            rhs_scale=w_scales[:, g, :],
+                            start=(g == 0),
+                            stop=(g == PASSES - 1),
+                        )
+                    by_head = acc[:].rearrange("p (h d) -> p h d", h=GROUP_HEADS)
+                    if section < 2:
+                        both = [P, 2, GROUP_HEADS, DH]
+                        nc.vector.tensor_tensor(
+                            out=product[:, j],
+                            in0=by_head.unsqueeze(1).to_broadcast(both),
+                            in1=tables[section][:, t].unsqueeze(2).to_broadcast(both),
+                            op=ALU.mult,
+                        )
+                    else:
+                        nc.scalar.copy(out=result[:, :, j, :], in_=by_head)
+                if section < 2:
+                    for lo in (0, HALF):
+                        partner = HALF - lo
+                        nc.gpsimd.tensor_tensor(
+                            out=result[:, :, :, lo : lo + HALF].rearrange("p h t d -> p t h d"),
+                            in0=product[:, :, 0, :, lo : lo + HALF],
+                            in1=product[:, :, 1, :, partner : partner + HALF],
+                            op=ALU.add,
+                        )
+                nc.sync.dma_start(
+                    out=out_view[:, first_head : first_head + GROUP_HEADS, t0 : t0 + T_RUN, :], in_=result[:]
+                )

@@ -182,7 +182,7 @@ def tile_ringattention_pa_kernel(tc, x, rotary_emb, gamma, w_qkv, out_q, out_k, 
                 if section < 2:
                     for lo in (0, HALF):
                         partner = HALF - lo
-                        nc.gpsimd.tensor_tensor(
+                        nc.vector.tensor_tensor(
                             out=result[:, :, :, lo : lo + HALF].rearrange("p h t d -> p t h d"),
                             in0=product[:, :, 0, :, lo : lo + HALF],
                             in1=product[:, :, 1, :, partner : partner + HALF],

@@ -28,6 +28,7 @@ ROW_TILES = SEQ // P
 N_COLS = 512
 GROUP_HEADS = N_COLS // DH
 T_RUN = 4
+T_RUN_LAST = 2
 
 GROUPS = ((0, 0), (0, 1), (2, 0), (1, 0), (2, 1), (1, 1))
 
@@ -42,11 +43,12 @@ def tile_ringattention_pa_kernel(tc, x, rotary_emb, gamma, w_qkv, out_q, out_k, 
         squares = ctx.enter_context(tc.tile_pool(name="squares", bufs=2))
         normed = ctx.enter_context(tc.tile_pool(name="normed", bufs=3))
         w_in = ctx.enter_context(tc.tile_pool(name="w_in", bufs=len(GROUPS)))
-        w_words = ctx.enter_context(tc.tile_pool(name="w_words", bufs=3))
+        w_words = ctx.enter_context(tc.tile_pool(name="w_words", bufs=2))
         w_mx = ctx.enter_context(tc.tile_pool(name="w_mx", bufs=3))
         products = ctx.enter_context(tc.tile_pool(name="products", bufs=3))
         results = ctx.enter_context(tc.tile_pool(name="results", bufs=4))
-        psum = ctx.enter_context(tc.psum_pool(name="psum", bufs=8))
+        psum_v = ctx.enter_context(tc.psum_pool(name="psum_v", bufs=5))
+        psum_s = ctx.enter_context(tc.psum_pool(name="psum_s", bufs=3))
 
         angles = keep.tile([P, ROW_TILES, DH], BF16)
         nc.sync.dma_start(out=angles[:], in_=rotary_emb.rearrange("(p t) d -> p t d", t=ROW_TILES))
@@ -86,11 +88,15 @@ def tile_ringattention_pa_kernel(tc, x, rotary_emb, gamma, w_qkv, out_q, out_k, 
         nc.scalar.activation(out=sin_half[:], in_=angles[:], func=ACT.Sin, scale=0.5)
         nc.scalar.activation(out=table_k[:, :, 1, 0:HALF], in_=angles[:, :, HALF:DH], func=ACT.Sin)
         nc.scalar.activation(out=table_k[:, :, 1, HALF:DH], in_=angles[:, :, 0:HALF], func=ACT.Sin, scale=-1.0)
+        nc.vector.tensor_tensor(out=sin_half[:], in0=sin_half[:], in1=sin_half[:], op=ALU.mult)
+        nc.vector.tensor_scalar(
+            out=table_k[:, :, 0, :], in0=sin_half[:], scalar1=-2.0, scalar2=1.0, op0=ALU.mult, op1=ALU.add
+        )
         tables = (table_q, table_k)
 
         gamma_all = keep.tile([P, DIM], BF16)
         for n in range(0, DIM, N_COLS):
-            spread = psum.tile([P, N_COLS], F32, tag="bank")
+            spread = psum_v.tile([P, N_COLS], F32, tag="bank")
             nc.tensor.matmul(out=spread[:], lhsT=ones[:], rhs=gamma_row[:, n : n + N_COLS], start=True, stop=True)
             nc.vector.tensor_copy(out=gamma_all[:, n : n + N_COLS], in_=spread[:])
 
@@ -117,7 +123,7 @@ def tile_ringattention_pa_kernel(tc, x, rotary_emb, gamma, w_qkv, out_q, out_k, 
                 out=xn[:], in0=x_rows[:, t, :], scalar=inv_rms[:, t : t + 1], in1=gamma_all[:],
                 op0=ALU.mult, op1=ALU.mult,
             )
-            xn_t = psum.tile([P, K_CHUNKS, P], BF16, tag="bank")
+            xn_t = psum_s.tile([P, K_CHUNKS, P], BF16, tag="bank")
             for c in range(K_CHUNKS):
                 nc.tensor.transpose(xn_t[:, c, :], xn[:, c * P : (c + 1) * P], ident[:])
             xn_words = normed.tile([P, PASSES, P, PACK], BF16, align_bytes=64)
@@ -128,36 +134,34 @@ def tile_ringattention_pa_kernel(tc, x, rotary_emb, gamma, w_qkv, out_q, out_k, 
                 in_=xn_words[:].rearrange("p g r u -> p (g r u)"),
             )
 
-        nc.vector.tensor_tensor(out=sin_half[:], in0=sin_half[:], in1=sin_half[:], op=ALU.mult)
-        nc.vector.tensor_scalar(
-            out=table_k[:, :, 0, :], in0=sin_half[:], scalar1=-2.0, scalar2=1.0, op0=ALU.mult, op1=ALU.add
-        )
         nc.vector.tensor_scalar_mul(out=table_q[:], in0=table_k[:], scalar1=math.sqrt(DH))
 
         for index, (section, half) in enumerate(GROUPS):
             w_codes = w_mx.tile([P, PASSES, N_COLS], U32, align_bytes=64)
             w_scales = w_mx.tile([P, PASSES, N_COLS], U8, align_bytes=64)
+            grouped = w_words.tile([P, PASSES, N_COLS, PACK], BF16, align_bytes=64)
+            regroup = nc.vector.tensor_copy if index == 0 else nc.scalar.copy
             for g in range(PASSES):
-                grouped = w_words.tile([P, N_COLS, PACK], BF16, align_bytes=64)
-                regroup = nc.vector.tensor_copy if index == 0 else nc.scalar.copy
                 regroup(
-                    out=grouped[:].rearrange("p (c i) u -> p c u i", i=4),
+                    out=grouped[:, g].rearrange("p (c i) u -> p c u i", i=4),
                     in_=w_raw[(section, half)][:, g * PACK : (g + 1) * PACK, :].rearrange("p u (c i) -> p c u i", i=4),
                 )
-                nc.vector.quantize_mx(
-                    out=w_codes[:, g, :].bitcast(FP8X4),
-                    scales=w_scales[:, g, :],
-                    in_=grouped[:].rearrange("p n u -> p (n u)"),
-                )
+            nc.vector.quantize_mx(
+                out=w_codes[:].rearrange("p g n -> p (g n)").bitcast(FP8X4),
+                scales=w_scales[:].rearrange("p g n -> p (g n)"),
+                in_=grouped[:].rearrange("p g n u -> p (g n u)"),
+            )
             out_view = outs[section][0].rearrange("h (p t) d -> p h t d", t=ROW_TILES)
             first_head = half * GROUP_HEADS
-            for t0 in range(0, ROW_TILES, T_RUN):
-                result = results.tile([P, GROUP_HEADS, T_RUN, DH], F32)
+            last_group = index == len(GROUPS) - 1
+            t_run = T_RUN_LAST if last_group else T_RUN
+            for t0 in range(0, ROW_TILES, t_run):
+                result = results.tile([P, GROUP_HEADS, t_run, DH], F32)
                 if section < 2:
-                    product = products.tile([P, T_RUN, 2, GROUP_HEADS, DH], F32)
-                for j in range(T_RUN):
+                    product = products.tile([P, t_run, 2, GROUP_HEADS, DH], F32)
+                for j in range(t_run):
                     t = t0 + j
-                    acc = psum.tile([P, N_COLS], F32, tag="bank")
+                    acc = (psum_v if section < 2 else psum_s).tile([P, N_COLS], F32, tag="bank", name="acc")
                     for g in range(PASSES):
                         nc.tensor.matmul_mx(
                             out=acc[:],
@@ -182,12 +186,13 @@ def tile_ringattention_pa_kernel(tc, x, rotary_emb, gamma, w_qkv, out_q, out_k, 
                 if section < 2:
                     for lo in (0, HALF):
                         partner = HALF - lo
-                        nc.vector.tensor_tensor(
+                        adder = nc.vector if last_group and lo == HALF else nc.gpsimd
+                        adder.tensor_tensor(
                             out=result[:, :, :, lo : lo + HALF].rearrange("p h t d -> p t h d"),
                             in0=product[:, :, 0, :, lo : lo + HALF],
                             in1=product[:, :, 1, :, partner : partner + HALF],
                             op=ALU.add,
                         )
                 nc.sync.dma_start(
-                    out=out_view[:, first_head : first_head + GROUP_HEADS, t0 : t0 + T_RUN, :], in_=result[:]
+                    out=out_view[:, first_head : first_head + GROUP_HEADS, t0 : t0 + t_run, :], in_=result[:]
                 )

@@ -66,13 +66,14 @@ def tile_ringattention_pa_kernel(tc, x, rotary_emb, gamma, w_qkv, out_q, out_k, 
         def load_w(section, half):
             first = (section * 2 + half) * N_COLS
             w_raw[(section, half)] = w_in.tile([P, K_CHUNKS, N_COLS], BF16, name="w_raw")
-            nc.sync.dma_start(out=w_raw[(section, half)][:], in_=w_view[:, :, first : first + N_COLS])
+            for c in range(0, K_CHUNKS, PACK):
+                nc.sync.dma_start(
+                    out=w_raw[(section, half)][:, c : c + PACK, :], in_=w_view[:, c : c + PACK, first : first + N_COLS]
+                )
 
-        load_x(0)
-        load_w(*GROUPS[0])
-        for t in range(2, ROW_TILES, 2):
+        for t in range(0, ROW_TILES, 2):
             load_x(t)
-        for section, half in GROUPS[1:]:
+        for section, half in GROUPS:
             load_w(section, half)
 
         ident = keep.tile([P, P], BF16)
@@ -136,21 +137,28 @@ def tile_ringattention_pa_kernel(tc, x, rotary_emb, gamma, w_qkv, out_q, out_k, 
 
         nc.vector.tensor_scalar_mul(out=table_q[:], in0=table_k[:], scalar1=math.sqrt(DH))
 
-        for index, (section, half) in enumerate(GROUPS):
-            w_codes = w_mx.tile([P, PASSES, N_COLS], U32, align_bytes=64)
-            w_scales = w_mx.tile([P, PASSES, N_COLS], U8, align_bytes=64)
-            grouped = w_words.tile([P, PASSES, N_COLS, PACK], BF16, align_bytes=64)
+        def quantise_weights(index):
+            codes = w_mx.tile([P, PASSES, N_COLS], U32, align_bytes=64, name="w_codes")
+            scales = w_mx.tile([P, PASSES, N_COLS], U8, align_bytes=64, name="w_scales")
+            grouped = w_words.tile([P, PASSES, N_COLS, PACK], BF16, align_bytes=64, name="grouped")
             regroup = nc.vector.tensor_copy if index == 0 else nc.scalar.copy
             for g in range(PASSES):
                 regroup(
                     out=grouped[:, g].rearrange("p (c i) u -> p c u i", i=4),
-                    in_=w_raw[(section, half)][:, g * PACK : (g + 1) * PACK, :].rearrange("p u (c i) -> p c u i", i=4),
+                    in_=w_raw[GROUPS[index]][:, g * PACK : (g + 1) * PACK, :].rearrange("p u (c i) -> p c u i", i=4),
                 )
             nc.vector.quantize_mx(
-                out=w_codes[:].rearrange("p g n -> p (g n)").bitcast(FP8X4),
-                scales=w_scales[:].rearrange("p g n -> p (g n)"),
+                out=codes[:].rearrange("p g n -> p (g n)").bitcast(FP8X4),
+                scales=scales[:].rearrange("p g n -> p (g n)"),
                 in_=grouped[:].rearrange("p g n u -> p (g n u)"),
             )
+            return codes, scales
+
+        ahead = quantise_weights(0)
+        for index, (section, half) in enumerate(GROUPS):
+            w_codes, w_scales = ahead
+            if index + 1 < len(GROUPS):
+                ahead = quantise_weights(index + 1)
             out_view = outs[section][0].rearrange("h (p t) d -> p h t d", t=ROW_TILES)
             first_head = half * GROUP_HEADS
             last_group = index == len(GROUPS) - 1

@@ -42,11 +42,12 @@ def tile_ringattention_pa_kernel(tc, x, rotary_emb, gamma, w_qkv, out_q, out_k, 
         keep = ctx.enter_context(tc.tile_pool(name="keep", bufs=1))
         squares = ctx.enter_context(tc.tile_pool(name="squares", bufs=2))
         normed = ctx.enter_context(tc.tile_pool(name="normed", bufs=3))
-        w_in = ctx.enter_context(tc.tile_pool(name="w_in", bufs=len(GROUPS)))
+        w_in = ctx.enter_context(tc.tile_pool(name="w_in", bufs=len(GROUPS) - 1))
         w_words = ctx.enter_context(tc.tile_pool(name="w_words", bufs=2))
         w_mx = ctx.enter_context(tc.tile_pool(name="w_mx", bufs=3))
         products = ctx.enter_context(tc.tile_pool(name="products", bufs=3))
-        results = ctx.enter_context(tc.tile_pool(name="results", bufs=4))
+        results = ctx.enter_context(tc.tile_pool(name="results", bufs=3))
+        results_v = ctx.enter_context(tc.tile_pool(name="results_v", bufs=2))
         psum_v = ctx.enter_context(tc.psum_pool(name="psum_v", bufs=5))
         psum_s = ctx.enter_context(tc.psum_pool(name="psum_s", bufs=3))
 
@@ -66,14 +67,13 @@ def tile_ringattention_pa_kernel(tc, x, rotary_emb, gamma, w_qkv, out_q, out_k, 
         def load_w(section, half):
             first = (section * 2 + half) * N_COLS
             w_raw[(section, half)] = w_in.tile([P, K_CHUNKS, N_COLS], BF16, name="w_raw")
-            for c in range(0, K_CHUNKS, PACK):
-                nc.sync.dma_start(
-                    out=w_raw[(section, half)][:, c : c + PACK, :], in_=w_view[:, c : c + PACK, first : first + N_COLS]
-                )
+            nc.sync.dma_start(out=w_raw[(section, half)][:], in_=w_view[:, :, first : first + N_COLS])
 
-        for t in range(0, ROW_TILES, 2):
+        load_x(0)
+        load_w(*GROUPS[0])
+        for t in range(2, ROW_TILES, 2):
             load_x(t)
-        for section, half in GROUPS:
+        for section, half in GROUPS[1:]:
             load_w(section, half)
 
         ident = keep.tile([P, P], BF16)
@@ -164,7 +164,7 @@ def tile_ringattention_pa_kernel(tc, x, rotary_emb, gamma, w_qkv, out_q, out_k, 
             last_group = index == len(GROUPS) - 1
             t_run = T_RUN_LAST if last_group else T_RUN
             for t0 in range(0, ROW_TILES, t_run):
-                result = results.tile([P, GROUP_HEADS, t_run, DH], F32)
+                result = (results if section < 2 else results_v).tile([P, GROUP_HEADS, t_run, DH], F32, name="result")
                 if section < 2:
                     product = products.tile([P, t_run, 2, GROUP_HEADS, DH], F32)
                 for j in range(t_run):
@@ -201,6 +201,7 @@ def tile_ringattention_pa_kernel(tc, x, rotary_emb, gamma, w_qkv, out_q, out_k, 
                             in1=product[:, :, 1, :, partner : partner + HALF],
                             op=ALU.add,
                         )
-                nc.sync.dma_start(
+                store_queue = nc.sync if section < 2 else nc.scalar
+                store_queue.dma_start(
                     out=out_view[:, first_head : first_head + GROUP_HEADS, t0 : t0 + t_run, :], in_=result[:]
                 )

@@ -194,7 +194,8 @@ def tile_ringattention_pa_kernel(tc, x, rotary_emb, gamma, w_qkv, out_q, out_k, 
                 if section < 2:
                     for lo in (0, HALF):
                         partner = HALF - lo
-                        adder = nc.vector if last_group and lo == HALF else nc.gpsimd
+                        last_run = t0 + t_run == ROW_TILES
+                        adder = nc.vector if lo == HALF and (last_run or last_group) else nc.gpsimd
                         adder.tensor_tensor(
                             out=result[:, :, :, lo : lo + HALF].rearrange("p h t d -> p t h d"),
                             in0=product[:, :, 0, :, lo : lo + HALF],

@@ -31,6 +31,8 @@ T_RUN = 4
 T_RUN_LAST = 2
 
 GROUPS = ((0, 0), (0, 1), (2, 0), (1, 0), (2, 1), (1, 1))
+LAST_ROTARY = (1, 1)
+AHEAD = 2
 
 FLOPS = 2 * SEQ * DIM * 3 * HEADS * DH
 
@@ -44,7 +46,7 @@ def tile_ringattention_pa_kernel(tc, x, rotary_emb, gamma, w_qkv, out_q, out_k, 
         normed = ctx.enter_context(tc.tile_pool(name="normed", bufs=3))
         w_in = ctx.enter_context(tc.tile_pool(name="w_in", bufs=len(GROUPS) - 1))
         w_words = ctx.enter_context(tc.tile_pool(name="w_words", bufs=2))
-        w_mx = ctx.enter_context(tc.tile_pool(name="w_mx", bufs=3))
+        w_mx = ctx.enter_context(tc.tile_pool(name="w_mx", bufs=AHEAD + 2))
         products = ctx.enter_context(tc.tile_pool(name="products", bufs=3))
         results = ctx.enter_context(tc.tile_pool(name="results", bufs=3))
         results_v = ctx.enter_context(tc.tile_pool(name="results_v", bufs=2))
@@ -154,14 +156,14 @@ def tile_ringattention_pa_kernel(tc, x, rotary_emb, gamma, w_qkv, out_q, out_k, 
             )
             return codes, scales
 
-        ahead = quantise_weights(0)
+        ready = [quantise_weights(index) for index in range(AHEAD)]
         for index, (section, half) in enumerate(GROUPS):
-            w_codes, w_scales = ahead
-            if index + 1 < len(GROUPS):
-                ahead = quantise_weights(index + 1)
+            if index + AHEAD < len(GROUPS):
+                ready.append(quantise_weights(index + AHEAD))
+            w_codes, w_scales = ready[index]
             out_view = outs[section][0].rearrange("h (p t) d -> p h t d", t=ROW_TILES)
             first_head = half * GROUP_HEADS
-            last_group = index == len(GROUPS) - 1
+            last_group = (section, half) == LAST_ROTARY
             t_run = T_RUN_LAST if last_group else T_RUN
             for t0 in range(0, ROW_TILES, t_run):
                 result = (results if section < 2 else results_v).tile([P, GROUP_HEADS, t_run, DH], F32, name="result")
@@ -194,8 +196,7 @@ def tile_ringattention_pa_kernel(tc, x, rotary_emb, gamma, w_qkv, out_q, out_k, 
                 if section < 2:
                     for lo in (0, HALF):
                         partner = HALF - lo
-                        last_run = t0 + t_run == ROW_TILES
-                        adder = nc.vector if lo == HALF and (last_run or last_group) else nc.gpsimd
+                        adder = nc.vector if last_group and lo == HALF else nc.gpsimd
                         adder.tensor_tensor(
                             out=result[:, :, :, lo : lo + HALF].rearrange("p h t d -> p t h d"),
                             in0=product[:, :, 0, :, lo : lo + HALF],

import math
from contextlib import ExitStack

import concourse.mybir as mybir
from concourse.masks import make_identity

FP8X4 = mybir.dt.float8_e4m3fn_x4
BF16 = mybir.dt.bfloat16
F32 = mybir.dt.float32
U32 = mybir.dt.uint32
U8 = mybir.dt.uint8
ACT = mybir.ActivationFunctionType
ALU = mybir.AluOpType

P = 128
SEQ = 1024
DIM = 1024
HEADS = 8
DH = 128
HALF = DH // 2
EPS = 1e-12

PACK = 4
K_PASS = P * PACK
PASSES = DIM // K_PASS
K_CHUNKS = DIM // P
ROW_TILES = SEQ // P
N_COLS = 512
GROUP_HEADS = N_COLS // DH
T_RUN = 4
T_RUN_LAST = 2

GROUPS = ((0, 0), (0, 1), (2, 0), (1, 0), (2, 1), (1, 1))
LAST_ROTARY = (1, 1)
AHEAD = 2

FLOPS = 2 * SEQ * DIM * 3 * HEADS * DH


def tile_ringattention_pa_kernel(tc, x, rotary_emb, gamma, w_qkv, out_q, out_k, out_v):
    nc = tc.nc
    outs = (out_q, out_k, out_v)
    with ExitStack() as ctx:
        keep = ctx.enter_context(tc.tile_pool(name="keep", bufs=1))
        squares = ctx.enter_context(tc.tile_pool(name="squares", bufs=2))
        normed = ctx.enter_context(tc.tile_pool(name="normed", bufs=3))
        w_in = ctx.enter_context(tc.tile_pool(name="w_in", bufs=len(GROUPS) - 1))
        w_words = ctx.enter_context(tc.tile_pool(name="w_words", bufs=2))
        w_mx = ctx.enter_context(tc.tile_pool(name="w_mx", bufs=AHEAD + 2))
        products = ctx.enter_context(tc.tile_pool(name="products", bufs=3))
        results = ctx.enter_context(tc.tile_pool(name="results", bufs=3))
        results_v = ctx.enter_context(tc.tile_pool(name="results_v", bufs=2))
        psum_v = ctx.enter_context(tc.psum_pool(name="psum_v", bufs=5))
        psum_s = ctx.enter_context(tc.psum_pool(name="psum_s", bufs=3))

        angles = keep.tile([P, ROW_TILES, DH], BF16)
        nc.sync.dma_start(out=angles[:], in_=rotary_emb.rearrange("(p t) d -> p t d", t=ROW_TILES))
        gamma_row = keep.tile([P, DIM], BF16)
        nc.vector.memset(gamma_row[:], 0.0)
        nc.sync.dma_start(out=gamma_row[0:1, :], in_=gamma.rearrange("(o k) -> o k", o=1))
        x_rows = keep.tile([P, ROW_TILES, DIM], BF16)
        x_view = x[0].rearrange("(p t) k -> p t k", t=ROW_TILES)
        w_view = w_qkv.rearrange("(c p) n -> p c n", p=P)
        w_raw = {}

        def load_x(t):
            nc.sync.dma_start(out=x_rows[:, t : t + 2, :], in_=x_view[:, t : t + 2, :])

        def load_w(section, half):
            first = (section * 2 + half) * N_COLS
            w_raw[(section, half)] = w_in.tile([P, K_CHUNKS, N_COLS], BF16, name="w_raw")
            nc.sync.dma_start(out=w_raw[(section, half)][:], in_=w_view[:, :, first : first + N_COLS])

        load_x(0)
        load_w(*GROUPS[0])
        for t in range(2, ROW_TILES, 2):
            load_x(t)
        for section, half in GROUPS[1:]:
            load_w(section, half)

        ident = keep.tile([P, P], BF16)
        make_identity(nc, ident[:])
        ones = keep.tile([P, P], BF16)
        nc.vector.memset(ones[:], 1.0)
        minus_half = keep.tile([P, ROW_TILES], F32)
        nc.gpsimd.memset(minus_half[:], -0.5)

        table_k = keep.tile([P, ROW_TILES, 2, DH], F32)
        table_q = keep.tile([P, ROW_TILES, 2, DH], F32)
        sin_half = keep.tile([P, ROW_TILES, DH], F32)
        nc.scalar.activation(out=sin_half[:], in_=angles[:], func=ACT.Sin, scale=0.5)
        nc.scalar.activation(out=table_k[:, :, 1, 0:HALF], in_=angles[:, :, HALF:DH], func=ACT.Sin)
        nc.scalar.activation(out=table_k[:, :, 1, HALF:DH], in_=angles[:, :, 0:HALF], func=ACT.Sin, scale=-1.0)
        nc.vector.tensor_tensor(out=sin_half[:], in0=sin_half[:], in1=sin_half[:], op=ALU.mult)
        nc.vector.tensor_scalar(
            out=table_k[:, :, 0, :], in0=sin_half[:], scalar1=-2.0, scalar2=1.0, op0=ALU.mult, op1=ALU.add
        )
        tables = (table_q, table_k)

        gamma_all = keep.tile([P, DIM], BF16)
        for n in range(0, DIM, N_COLS):
            spread = psum_v.tile([P, N_COLS], F32, tag="bank")
            nc.tensor.matmul(out=spread[:], lhsT=ones[:], rhs=gamma_row[:, n : n + N_COLS], start=True, stop=True)
            nc.vector.tensor_copy(out=gamma_all[:, n : n + N_COLS], in_=spread[:])

        x_codes = keep.tile([P, ROW_TILES, PASSES, P], U32, align_bytes=64)
        x_scales = keep.tile([P, ROW_TILES, PASSES, P], U8, align_bytes=64)
        mean_sq = keep.tile([P, ROW_TILES], F32)
        floored = keep.tile([P, ROW_TILES], F32)
        inv_rms = keep.tile([P, ROW_TILES], F32)
        for t in range(ROW_TILES):
            sq = squares.tile([P, DIM], BF16)
            nc.scalar.activation(
                out=sq[:], in_=x_rows[:, t, :], func=ACT.Square, scale=1.0 / math.sqrt(DIM),
                accum_out=mean_sq[:, t : t + 1],
            )
            nc.gpsimd.tensor_scalar(
                out=floored[:, t : t + 1], in0=mean_sq[:, t : t + 1], scalar1=EPS * EPS / DIM, scalar2=None,
                op0=ALU.max,
            )
            nc.gpsimd.tensor_tensor(
                out=inv_rms[:, t : t + 1], in0=floored[:, t : t + 1], in1=minus_half[:, t : t + 1], op=ALU.pow
            )
            xn = normed.tile([P, DIM], BF16)
            nc.vector.scalar_tensor_tensor(
                out=xn[:], in0=x_rows[:, t, :], scalar=inv_rms[:, t : t + 1], in1=gamma_all[:],
                op0=ALU.mult, op1=ALU.mult,
            )
            xn_t = psum_s.tile([P, K_CHUNKS, P], BF16, tag="bank")
            for c in range(K_CHUNKS):
                nc.tensor.transpose(xn_t[:, c, :], xn[:, c * P : (c + 1) * P], ident[:])
            xn_words = normed.tile([P, PASSES, P, PACK], BF16, align_bytes=64)
            nc.scalar.copy(out=xn_words[:], in_=xn_t[:].rearrange("p (g u) r -> p g r u", u=PACK))
            nc.vector.quantize_mx(
                out=x_codes[:, t].rearrange("p g r -> p (g r)").bitcast(FP8X4),
                scales=x_scales[:, t].rearrange("p g r -> p (g r)"),
                in_=xn_words[:].rearrange("p g r u -> p (g r u)"),
            )

        nc.vector.tensor_scalar_mul(out=table_q[:], in0=table_k[:], scalar1=math.sqrt(DH))

        def quantise_weights(index):
            codes = w_mx.tile([P, PASSES, N_COLS], U32, align_bytes=64, name="w_codes")
            scales = w_mx.tile([P, PASSES, N_COLS], U8, align_bytes=64, name="w_scales")
            grouped = w_words.tile([P, PASSES, N_COLS, PACK], BF16, align_bytes=64, name="grouped")
            regroup = nc.vector.tensor_copy if index == 0 else nc.scalar.copy
            for g in range(PASSES):
                regroup(
                    out=grouped[:, g].rearrange("p (c i) u -> p c u i", i=4),
                    in_=w_raw[GROUPS[index]][:, g * PACK : (g + 1) * PACK, :].rearrange("p u (c i) -> p c u i", i=4),
                )
            nc.vector.quantize_mx(
                out=codes[:].rearrange("p g n -> p (g n)").bitcast(FP8X4),
                scales=scales[:].rearrange("p g n -> p (g n)"),
                in_=grouped[:].rearrange("p g n u -> p (g n u)"),
            )
            return codes, scales

        ready = [quantise_weights(index) for index in range(AHEAD)]
        for index, (section, half) in enumerate(GROUPS):
            if index + AHEAD < len(GROUPS):
                ready.append(quantise_weights(index + AHEAD))
            w_codes, w_scales = ready[index]
            out_view = outs[section][0].rearrange("h (p t) d -> p h t d", t=ROW_TILES)
            first_head = half * GROUP_HEADS
            last_group = (section, half) == LAST_ROTARY
            t_run = T_RUN_LAST if last_group else T_RUN
            for t0 in range(0, ROW_TILES, t_run):
                result = (results if section < 2 else results_v).tile([P, GROUP_HEADS, t_run, DH], F32, name="result")
                if section < 2:
                    product = products.tile([P, t_run, 2, GROUP_HEADS, DH], F32)
                for j in range(t_run):
                    t = t0 + j
                    acc = (psum_v if section < 2 else psum_s).tile([P, N_COLS], F32, tag="bank", name="acc")
                    for g in range(PASSES):
                        nc.tensor.matmul_mx(
                            out=acc[:],
                            lhsT=x_codes[:, t, g, :].bitcast(FP8X4),
                            lhsT_scale=x_scales[:, t, g, :],
                            rhs=w_codes[:, g, :].bitcast(FP8X4),
                            rhs_scale=w_scales[:, g, :],
                            start=(g == 0),
                            stop=(g == PASSES - 1),
                        )
                    by_head = acc[:].rearrange("p (h d) -> p h d", h=GROUP_HEADS)
                    if section < 2:
                        both = [P, 2, GROUP_HEADS, DH]
                        nc.vector.tensor_tensor(
                            out=product[:, j],
                            in0=by_head.unsqueeze(1).to_broadcast(both),
                            in1=tables[section][:, t].unsqueeze(2).to_broadcast(both),
                            op=ALU.mult,
                        )
                    else:
                        nc.scalar.copy(out=result[:, :, j, :], in_=by_head)
                if section < 2:
                    for lo in (0, HALF):
                        partner = HALF - lo
                        adder = nc.vector if last_group and lo == HALF else nc.gpsimd
                        adder.tensor_tensor(
                            out=result[:, :, :, lo : lo + HALF].rearrange("p h t d -> p t h d"),
                            in0=product[:, :, 0, :, lo : lo + HALF],
                            in1=product[:, :, 1, :, partner : partner + HALF],
                            op=ALU.add,
                        )
                store_queue = nc.sync if section < 2 else nc.scalar
                store_queue.dma_start(
                    out=out_view[:, first_head : first_head + GROUP_HEADS, t0 : t0 + t_run, :], in_=result[:]
                )
